import numpy as np
import ml_dtypes


def mxq(x, axis, fmt="e4m3"):
    dtype, down = {"e4m3": (ml_dtypes.float8_e4m3fn, 7), "e5m2": (ml_dtypes.float8_e5m2, 14)}[fmt]
    v = np.moveaxis(np.asarray(x, np.float32).astype(ml_dtypes.bfloat16).astype(np.float64), axis, -1)
    blocks = v.reshape(v.shape[:-1] + (-1, 32))
    amax = np.abs(blocks).max(-1, keepdims=True)
    byte = np.maximum(np.where(amax > 0, np.frexp(amax)[1] - 1 + 127, 0) - down, 1)
    scale = np.exp2(byte - 127.0)
    codes = (blocks / scale).astype(np.float32).astype(dtype).astype(np.float64)
    return np.moveaxis((codes * scale).reshape(v.shape), -1, axis)


WIDE = False


def mx_kscale(k):
    if not WIDE:
        return np.ones(k)
    levels = np.array([10, -10, 5, -5, 0])
    a = np.random.permutation(np.resize(levels, k // 512 * 4)).reshape(k // 512, 4)
    idx = np.arange(k)
    return np.exp2(a[idx // 512, idx % 128 // 32])


BF16 = ml_dtypes.bfloat16


def bf(x):
    return np.asarray(x, np.float32).astype(BF16)


def f64(x):
    return np.asarray(x).astype(np.float64)


E2M1 = np.array([0.0, 0.5, 1.0, 1.5, 2.0, 3.0, 4.0, 6.0, -0.0, -0.5, -1.0, -1.5, -2.0, -3.0, -4.0, -6.0])


def pack_weight(w, fmt):
    k, n = w.shape
    w = f64(bf(w)).reshape(k // 32, 32, n)
    amax = np.abs(w).max(1)
    if fmt == "e4m3":
        byte = np.frexp(amax)[1] - 1 + 127 - 7
    else:
        mant, ex = np.frexp(amax / 6.0)
        byte = np.where(mant > 0.5, ex, ex - 1) + 127
    byte = np.clip(np.where(amax > 0, byte, 1), 1, 254)
    scaled = (w * np.exp2(127.0 - byte)[:, None, :]).reshape(k, n).astype(np.float32)
    by_word = np.ascontiguousarray(scaled.reshape(k // 512, 128, 4, n).transpose(0, 1, 3, 2))
    if fmt == "e4m3":
        words = by_word.astype(ml_dtypes.float8_e4m3fn).view(np.uint8)
    else:
        c = by_word.astype(ml_dtypes.float4_e2m1fn).view(np.uint8) & 0xF
        words = c[..., 0::2] | (c[..., 1::2] << 4)
    return np.ascontiguousarray(words), np.ascontiguousarray(byte.astype(np.uint8).reshape(k // 512, 16, n))


def unpack_weight(words, scales, fmt):
    g, p, n, _ = words.shape
    if fmt == "e4m3":
        vals = np.ascontiguousarray(words).view(ml_dtypes.float8_e4m3fn).astype(np.float64)
    else:
        nib = np.empty((g, p, n, 4), np.uint8)
        nib[..., 0::2] = words & 0xF
        nib[..., 1::2] = words >> 4
        vals = E2M1[nib]
    vals = vals * np.repeat(np.exp2(scales.astype(np.float64) - 127.0), 8, axis=1)[..., None]
    return vals.transpose(0, 1, 3, 2).reshape(g * 512, n)


B, N, D, H, HD, FF = 2, 512, 1024, 8, 128, 4096
E = H * HD
EPS = 1e-5
FMT = "e4m3"


def layernorm(x, gamma, beta):
    mu = x.mean(-1, keepdims=True)
    var = ((x - mu) ** 2).mean(-1, keepdims=True)
    return (x - mu) * (1.0 / np.sqrt(var + EPS)) * gamma + beta


def heads(y):
    return y.reshape(B, N, H, HD).transpose(0, 2, 1, 3)


def setup_inputs():
    s = mx_kscale(D)
    r = np.random.standard_normal
    x = bf(r((B, N, D)))
    gamma = bf((1.0 + 0.1 * r(D)) * s)
    beta = bf(0.1 * r(D) * s)
    Wq_words, Wq_scales = pack_weight(r((D, E)) * 1.4 / np.sqrt(D) / s[:, None], FMT)
    bq = bf(r(E) * 0.2)
    Wk_words, Wk_scales = pack_weight(r((D, E)) * 1.4 / np.sqrt(D) / s[:, None], FMT)
    bk = bf(r(E) * 0.2)
    Wv_words, Wv_scales = pack_weight(r((D, E)) * 1.0 / np.sqrt(D) / s[:, None], FMT)
    bv = bf(r(E) * 0.2)
    return {"x": x,
            "gamma": gamma, "beta": beta,
            "Wq_words": Wq_words, "Wq_scales": Wq_scales, "bq": bq,
            "Wk_words": Wk_words, "Wk_scales": Wk_scales, "bk": bk,
            "Wv_words": Wv_words, "Wv_scales": Wv_scales, "bv": bv}


def reference(x, gamma, beta, Wq_words, Wq_scales, bq, Wk_words, Wk_scales, bk, Wv_words, Wv_scales, bv):
    h = layernorm(f64(x), f64(gamma), f64(beta))
    hq = mxq(h, 2, "e4m3")
    q = (hq @ unpack_weight(Wq_words, Wq_scales, FMT)) + f64(bq)
    k = (hq @ unpack_weight(Wk_words, Wk_scales, FMT)) + f64(bk)
    v = (hq @ unpack_weight(Wv_words, Wv_scales, FMT)) + f64(bv)
    return heads(q), heads(k), heads(v)

@@ -1,0 +1,200 @@
+from contextlib import ExitStack
+
+import concourse.mybir as mybir
+from concourse.masks import make_identity
+
+F32 = mybir.dt.float32
+BF16 = mybir.dt.bfloat16
+I32 = mybir.dt.int32
+U32 = mybir.dt.uint32
+U8 = mybir.dt.uint8
+FP8X4 = mybir.dt.float8_e4m3fn_x4
+ALU = mybir.AluOpType
+ACT = mybir.ActivationFunctionType
+
+P = 128
+BATCHES = 2
+TOKENS = 512
+FEATURES = 1024
+COLUMNS = 1024
+HEAD = 128
+EPS = 1e-5
+PACK = 4
+K_PASS = P * PACK
+PASSES = FEATURES // K_PASS
+TILES = TOKENS // P
+BANK = 512
+BANK_HEADS = BANK // HEAD
+GROUPS = COLUMNS // BANK
+STATS_MAX = 512
+STATS_DIM = 6
+
+FLOPS = 2 * BATCHES * TOKENS * FEATURES * 3 * COLUMNS
+
+
+def tile_vit_transformerblock_pa_kernel(
+    tc, x, gamma, beta, Wq_words, Wq_scales, bq, Wk_words, Wk_scales, bk, Wv_words, Wv_scales, bv,
+    out_0, out_1, out_2,
+):
+    nc = tc.nc
+    weights = ((Wq_words, Wq_scales, bq, out_0), (Wk_words, Wk_scales, bk, out_1), (Wv_words, Wv_scales, bv, out_2))
+    n_weights = len(weights)
+
+    with ExitStack() as ctx:
+        keep = ctx.enter_context(tc.tile_pool(name="keep", bufs=1))
+        norm = ctx.enter_context(tc.tile_pool(name="norm", bufs=BATCHES))
+        results = ctx.enter_context(tc.tile_pool(name="results", bufs=4))
+        banks = ctx.enter_context(tc.psum_pool(name="banks", bufs=8))
+
+        eps = keep.tile([P, 1], F32)
+        nc.vector.memset(eps[:], EPS)
+        bias_rows = keep.tile([P, n_weights, COLUMNS], BF16)
+        nc.vector.memset(bias_rows[:].bitcast(I32), 0)
+        w_scales = keep.tile([P, n_weights, PASSES, COLUMNS], U8, align_bytes=64)
+        nc.vector.memset(w_scales[:].bitcast(I32), 0)
+        ones = keep.tile([P, P], BF16)
+        nc.vector.memset(ones[:], 1.0)
+        identity = keep.tile([P, P], F32)
+        make_identity(nc, identity[:])
+
+        x_sb = keep.tile([P, BATCHES, TILES, FEATURES], BF16)
+        for b in range(BATCHES):
+            x_tiles = x[b].rearrange("(p j) f -> j p f", j=TILES)
+            for j in range(TILES):
+                nc.sync.dma_start(out=x_sb[:, b, j, :], in_=x_tiles[j])
+
+        gamma_bf = keep.tile([P, PASSES, PACK], BF16)
+        beta_bf = keep.tile([P, PASSES, PACK], BF16)
+        nc.scalar.dma_start(out=gamma_bf[:], in_=gamma.rearrange("(g p t) -> p g t", g=PASSES, t=PACK))
+        nc.scalar.dma_start(out=beta_bf[:], in_=beta.rearrange("(g p t) -> p g t", g=PASSES, t=PACK))
+        table_warm = keep.tile([P, 1], F32)
+        nc.scalar.activation(out=table_warm[:], in_=eps[:], func=ACT.Sqrt)
+        for w in range(n_weights):
+            nc.scalar.dma_start(out=bias_rows[0:1, w, :], in_=weights[w][2].rearrange("(o n) -> o n", o=1))
+
+        for w in range(n_weights):
+            for quadrant in range(4):
+                rows = slice(4 * quadrant, 4 * quadrant + 4)
+                nc.sync.dma_start(
+                    out=w_scales[32 * quadrant : 32 * quadrant + 4, w, :, :].bitcast(I32),
+                    in_=weights[w][1][:, rows, :].rearrange("g r n -> r g n").bitcast(I32),
+                )
+        w_words = keep.tile([P, n_weights, PASSES, COLUMNS], U32, align_bytes=64)
+        for w in range(n_weights):
+            nc.sync.dma_start(
+                out=w_words[:, w, :, :].bitcast(I32),
+                in_=weights[w][0].rearrange("g p n t -> p g (n t)").bitcast(I32),
+            )
+
+        gamma_f = keep.tile([P, PASSES, PACK], F32)
+        beta_f = keep.tile([P, PASSES, PACK], F32)
+        bias_all = keep.tile([P, n_weights, COLUMNS], F32)
+        h_words = keep.tile([P, BATCHES, PASSES, TOKENS], U32, align_bytes=64)
+        h_scales = keep.tile([P, BATCHES, PASSES, TOKENS], U8, align_bytes=64)
+        standardised = {}
+        planes_of = {}
+        grouped_of = {}
+
+        def standardise_batch(b):
+            stats = norm.tile([P, TILES, FEATURES // STATS_MAX, STATS_DIM], F32)
+            mean_var = norm.tile([P, TILES, 2], F32)
+            std = norm.tile([P, TILES], F32)
+            rstd = norm.tile([P, TILES], F32)
+            shift = norm.tile([P, TILES], F32)
+            z = norm.tile([P, TILES, PACK, FEATURES // PACK], F32)
+            standardised[b] = z
+            for j in range(TILES):
+                for s in range(FEATURES // STATS_MAX):
+                    nc.vector.bn_stats(out=stats[:, j, s, :], in_=x_sb[:, b, j, s * STATS_MAX : (s + 1) * STATS_MAX])
+                nc.vector.bn_aggr(out=mean_var[:, j, :], in_=stats[:, j, :, :].rearrange("p s v -> p (s v)"))
+                nc.scalar.activation(out=std[:, j : j + 1], in_=mean_var[:, j, 1:2], func=ACT.Sqrt, bias=eps[:], scale=1.0)
+                nc.vector.reciprocal(out=rstd[:, j : j + 1], in_=std[:, j : j + 1])
+                nc.vector.scalar_tensor_tensor(
+                    out=shift[:, j : j + 1], in0=mean_var[:, j, 0:1], scalar=-1.0, in1=rstd[:, j : j + 1],
+                    op0=ALU.mult, op1=ALU.mult,
+                )
+                nc.scalar.activation(
+                    out=z[:, j, :, :], in_=x_sb[:, b, j, :].rearrange("p (c t) -> p t c", t=PACK),
+                    func=ACT.Identity, scale=rstd[:, j : j + 1], bias=shift[:, j : j + 1],
+                )
+
+        def to_mx_operand(b, g):
+            z = standardised[b]
+            if g == 0:
+                planes = norm.tile([P, PASSES, PACK, TOKENS], BF16)
+                grouped = norm.tile([P, PASSES, TOKENS, PACK], BF16, align_bytes=64)
+                planes_of[b] = planes
+                grouped_of[b] = grouped
+            planes = planes_of[b]
+            grouped = grouped_of[b]
+            for t in range(PACK):
+                bank = banks.tile([P, TILES, P], F32, tag="bank")
+                for j in range(TILES):
+                    nc.tensor.transpose(bank[:, j, :], z[:, j, t, g * P : (g + 1) * P], identity[:])
+                nc.scalar.activation(
+                    out=planes[:, g, t, :], in_=bank[:].rearrange("p j m -> p (j m)"), func=ACT.Identity,
+                    scale=gamma_f[:, g, t : t + 1], bias=beta_f[:, g, t : t + 1],
+                )
+            nc.vector.tensor_copy(
+                out=grouped[:, g, :, :].rearrange("p (c i) t -> p c t i", i=4),
+                in_=planes[:, g, :, :].rearrange("p t (c i) -> p c t i", i=4),
+            )
+            nc.vector.quantize_mx(
+                out=h_words[:, b, g, :].bitcast(FP8X4),
+                scales=h_scales[:, b, g, :],
+                in_=grouped[:, g, :, :].rearrange("p c t -> p (c t)"),
+            )
+
+        def broadcast_biases():
+            for w in range(n_weights):
+                for group in range(GROUPS):
+                    cols = slice(group * BANK, (group + 1) * BANK)
+                    bank = banks.tile([P, BANK], F32, tag="bank")
+                    nc.tensor.matmul(out=bank[:], lhsT=ones[:], rhs=bias_rows[:, w, cols], start=True, stop=True)
+                    nc.scalar.copy(out=bias_all[:, w, cols], in_=bank[:])
+
+        def project(b, w, group):
+            cols = slice(group * BANK, (group + 1) * BANK)
+            result = results.tile([P, BANK_HEADS, TILES, HEAD], F32)
+            for j in range(TILES):
+                tokens = slice(j * P, (j + 1) * P)
+                bank = banks.tile([P, BANK], F32, tag="bank")
+                for g in range(PASSES):
+                    nc.tensor.matmul_mx(
+                        out=bank[:],
+                        lhsT=h_words[:, b, g, tokens].bitcast(FP8X4),
+                        lhsT_scale=h_scales[:, b, g, tokens],
+                        rhs=w_words[:, w, g, cols].bitcast(FP8X4),
+                        rhs_scale=w_scales[:, w, g, cols],
+                        start=(g == 0),
+                        stop=(g == PASSES - 1),
+                    )
+                sums = bank[:].rearrange("p (a d) -> p a d", d=HEAD)
+                bias = bias_all[:, w, cols].rearrange("p (a d) -> p a d", d=HEAD)
+                if j == 0:
+                    nc.scalar.copy(out=result[:, :, j, :], in_=sums)
+                    nc.gpsimd.tensor_tensor(out=result[:, :, j, :], in0=result[:, :, j, :], in1=bias, op=ALU.add)
+                else:
+                    nc.vector.tensor_tensor(out=result[:, :, j, :], in0=sums, in1=bias, op=ALU.add)
+            heads = slice(group * BANK_HEADS, (group + 1) * BANK_HEADS)
+            nc.sync.dma_start(
+                out=weights[w][3][b, heads].rearrange("a (p j) d -> p a (j d)", j=TILES),
+                in_=result[:].rearrange("p a j d -> p a (j d)"),
+            )
+
+        units = [(w, group) for w in range(n_weights) for group in range(GROUPS)]
+
+        standardise_batch(0)
+        nc.vector.tensor_copy(out=gamma_f[:], in_=gamma_bf[:])
+        nc.vector.tensor_copy(out=beta_f[:], in_=beta_bf[:])
+        to_mx_operand(0, 0)
+        to_mx_operand(0, 1)
+        broadcast_biases()
+        for step, (w, group) in enumerate(units):
+            project(0, w, group)
+            if step == 0:
+                standardise_batch(1)
+            elif step <= PASSES:
+                to_mx_operand(1, step - 1)
+        for w, group in units:
+            project(1, w, group)

@@ -45,6 +45,7 @@ def tile_vit_transformerblock_pa_kernel(
         norm = ctx.enter_context(tc.tile_pool(name="norm", bufs=BATCHES))
         results = ctx.enter_context(tc.tile_pool(name="results", bufs=4))
         banks = ctx.enter_context(tc.psum_pool(name="banks", bufs=8))
+        ctx.enter_context(tc.manual_schedule())
 
         eps = keep.tile([P, 1], F32)
         nc.vector.memset(eps[:], EPS)
@@ -72,6 +73,7 @@ def tile_vit_transformerblock_pa_kernel(
         for w in range(n_weights):
             nc.scalar.dma_start(out=bias_rows[0:1, w, :], in_=weights[w][2].rearrange("(o n) -> o n", o=1))
 
+        w_words = keep.tile([P, n_weights, PASSES, COLUMNS], U32, align_bytes=64)
         for w in range(n_weights):
             for quadrant in range(4):
                 rows = slice(4 * quadrant, 4 * quadrant + 4)
@@ -79,8 +81,6 @@ def tile_vit_transformerblock_pa_kernel(
                     out=w_scales[32 * quadrant : 32 * quadrant + 4, w, :, :].bitcast(I32),
                     in_=weights[w][1][:, rows, :].rearrange("g r n -> r g n").bitcast(I32),
                 )
-        w_words = keep.tile([P, n_weights, PASSES, COLUMNS], U32, align_bytes=64)
-        for w in range(n_weights):
             nc.sync.dma_start(
                 out=w_words[:, w, :, :].bitcast(I32),
                 in_=weights[w][0].rearrange("g p n t -> p g (n t)").bitcast(I32),
@@ -91,70 +91,79 @@ def tile_vit_transformerblock_pa_kernel(
         bias_all = keep.tile([P, n_weights, COLUMNS], F32)
         h_words = keep.tile([P, BATCHES, PASSES, TOKENS], U32, align_bytes=64)
         h_scales = keep.tile([P, BATCHES, PASSES, TOKENS], U8, align_bytes=64)
-        standardised = {}
-        planes_of = {}
-        grouped_of = {}
 
-        def standardise_batch(b):
+        def batch_tiles():
             stats = norm.tile([P, TILES, FEATURES // STATS_MAX, STATS_DIM], F32)
             mean_var = norm.tile([P, TILES, 2], F32)
             std = norm.tile([P, TILES], F32)
             rstd = norm.tile([P, TILES], F32)
             shift = norm.tile([P, TILES], F32)
             z = norm.tile([P, TILES, PACK, FEATURES // PACK], F32)
-            standardised[b] = z
-            for j in range(TILES):
-                for s in range(FEATURES // STATS_MAX):
-                    nc.vector.bn_stats(out=stats[:, j, s, :], in_=x_sb[:, b, j, s * STATS_MAX : (s + 1) * STATS_MAX])
-                nc.vector.bn_aggr(out=mean_var[:, j, :], in_=stats[:, j, :, :].rearrange("p s v -> p (s v)"))
-                nc.scalar.activation(out=std[:, j : j + 1], in_=mean_var[:, j, 1:2], func=ACT.Sqrt, bias=eps[:], scale=1.0)
-                nc.vector.reciprocal(out=rstd[:, j : j + 1], in_=std[:, j : j + 1])
-                nc.vector.scalar_tensor_tensor(
-                    out=shift[:, j : j + 1], in0=mean_var[:, j, 0:1], scalar=-1.0, in1=rstd[:, j : j + 1],
-                    op0=ALU.mult, op1=ALU.mult,
-                )
-                nc.scalar.activation(
-                    out=z[:, j, :, :], in_=x_sb[:, b, j, :].rearrange("p (c t) -> p t c", t=PACK),
-                    func=ACT.Identity, scale=rstd[:, j : j + 1], bias=shift[:, j : j + 1],
-                )
+            planes = norm.tile([P, PASSES, PACK, TOKENS], BF16)
+            grouped = norm.tile([P, PASSES, TOKENS, PACK], BF16, align_bytes=64)
+            return dict(stats=stats, mean_var=mean_var, std=std, rstd=rstd, shift=shift, z=z, planes=planes, grouped=grouped)
 
-        def to_mx_operand(b, g):
-            z = standardised[b]
-            if g == 0:
-                planes = norm.tile([P, PASSES, PACK, TOKENS], BF16)
-                grouped = norm.tile([P, PASSES, TOKENS, PACK], BF16, align_bytes=64)
-                planes_of[b] = planes
-                grouped_of[b] = grouped
-            planes = planes_of[b]
-            grouped = grouped_of[b]
+        of_batch = [batch_tiles() for b in range(BATCHES)]
+        every_tile = slice(0, TILES)
+
+        def moments(b, j):
+            t = of_batch[b]
+            for s in range(FEATURES // STATS_MAX):
+                nc.vector.bn_stats(out=t["stats"][:, j, s, :], in_=x_sb[:, b, j, s * STATS_MAX : (s + 1) * STATS_MAX])
+            nc.vector.bn_aggr(out=t["mean_var"][:, j, :], in_=t["stats"][:, j, :, :].rearrange("p s v -> p (s v)"))
+
+        def root(b, tiles):
+            t = of_batch[b]
+            nc.scalar.activation(out=t["std"][:, tiles], in_=t["mean_var"][:, tiles, 1], func=ACT.Sqrt, bias=eps[:], scale=1.0)
+
+        def scale_and_shift(b, tiles):
+            t = of_batch[b]
+            nc.vector.reciprocal(out=t["rstd"][:, tiles], in_=t["std"][:, tiles])
+            nc.vector.scalar_tensor_tensor(
+                out=t["shift"][:, tiles], in0=t["mean_var"][:, tiles, 0], scalar=-1.0, in1=t["rstd"][:, tiles],
+                op0=ALU.mult, op1=ALU.mult,
+            )
+
+        def standardise(b, j):
+            t = of_batch[b]
+            nc.scalar.activation(
+                out=t["z"][:, j, :, :], in_=x_sb[:, b, j, :].rearrange("p (c t) -> p t c", t=PACK),
+                func=ACT.Identity, scale=t["rstd"][:, j : j + 1], bias=t["shift"][:, j : j + 1],
+            )
+
+        def transpose_scale(b, g):
+            tiles = of_batch[b]
             for t in range(PACK):
                 bank = banks.tile([P, TILES, P], F32, tag="bank")
                 for j in range(TILES):
-                    nc.tensor.transpose(bank[:, j, :], z[:, j, t, g * P : (g + 1) * P], identity[:])
+                    nc.tensor.transpose(bank[:, j, :], tiles["z"][:, j, t, g * P : (g + 1) * P], identity[:])
                 nc.scalar.activation(
-                    out=planes[:, g, t, :], in_=bank[:].rearrange("p j m -> p (j m)"), func=ACT.Identity,
+                    out=tiles["planes"][:, g, t, :], in_=bank[:].rearrange("p j m -> p (j m)"), func=ACT.Identity,
                     scale=gamma_f[:, g, t : t + 1], bias=beta_f[:, g, t : t + 1],
                 )
+
+        def quantise(b, g):
+            tiles = of_batch[b]
             nc.vector.tensor_copy(
-                out=grouped[:, g, :, :].rearrange("p (c i) t -> p c t i", i=4),
-                in_=planes[:, g, :, :].rearrange("p t (c i) -> p c t i", i=4),
+                out=tiles["grouped"][:, g, :, :].rearrange("p (c i) t -> p c t i", i=4),
+                in_=tiles["planes"][:, g, :, :].rearrange("p t (c i) -> p c t i", i=4),
             )
             nc.vector.quantize_mx(
                 out=h_words[:, b, g, :].bitcast(FP8X4),
                 scales=h_scales[:, b, g, :],
-                in_=grouped[:, g, :, :].rearrange("p c t -> p (c t)"),
+                in_=tiles["grouped"][:, g, :, :].rearrange("p c t -> p (c t)"),
             )
 
-        def broadcast_biases():
-            for w in range(n_weights):
-                for group in range(GROUPS):
-                    cols = slice(group * BANK, (group + 1) * BANK)
-                    bank = banks.tile([P, BANK], F32, tag="bank")
-                    nc.tensor.matmul(out=bank[:], lhsT=ones[:], rhs=bias_rows[:, w, cols], start=True, stop=True)
-                    nc.scalar.copy(out=bias_all[:, w, cols], in_=bank[:])
+        def broadcast_bias(w):
+            for group in range(GROUPS):
+                cols = slice(group * BANK, (group + 1) * BANK)
+                bank = banks.tile([P, BANK], F32, tag="bank")
+                nc.tensor.matmul(out=bank[:], lhsT=ones[:], rhs=bias_rows[:, w, cols], start=True, stop=True)
+                nc.scalar.copy(out=bias_all[:, w, cols], in_=bank[:])
 
         def project(b, w, group):
             cols = slice(group * BANK, (group + 1) * BANK)
+            bias = bias_all[:, w, cols].rearrange("p (a d) -> p a d", d=HEAD)
             result = results.tile([P, BANK_HEADS, TILES, HEAD], F32)
             for j in range(TILES):
                 tokens = slice(j * P, (j + 1) * P)
@@ -170,7 +179,6 @@ def tile_vit_transformerblock_pa_kernel(
                         stop=(g == PASSES - 1),
                     )
                 sums = bank[:].rearrange("p (a d) -> p a d", d=HEAD)
-                bias = bias_all[:, w, cols].rearrange("p (a d) -> p a d", d=HEAD)
                 if j == 0:
                     nc.scalar.copy(out=result[:, :, j, :], in_=sums)
                     nc.gpsimd.tensor_tensor(out=result[:, :, j, :], in0=result[:, :, j, :], in1=bias, op=ALU.add)
@@ -182,19 +190,42 @@ def tile_vit_transformerblock_pa_kernel(
                 in_=result[:].rearrange("p a j d -> p a (j d)"),
             )
 
-        units = [(w, group) for w in range(n_weights) for group in range(GROUPS)]
-
-        standardise_batch(0)
+        for j in range(TILES + 1):
+            if j < TILES:
+                moments(0, j)
+                root(0, slice(j, j + 1))
+            if j > 0:
+                scale_and_shift(0, slice(j - 1, j))
+                standardise(0, j - 1)
         nc.vector.tensor_copy(out=gamma_f[:], in_=gamma_bf[:])
         nc.vector.tensor_copy(out=beta_f[:], in_=beta_bf[:])
-        to_mx_operand(0, 0)
-        to_mx_operand(0, 1)
-        broadcast_biases()
-        for step, (w, group) in enumerate(units):
-            project(0, w, group)
-            if step == 0:
-                standardise_batch(1)
-            elif step <= PASSES:
-                to_mx_operand(1, step - 1)
-        for w, group in units:
-            project(1, w, group)
+        for j in range(TILES):
+            moments(1, j)
+        transpose_scale(0, 0)
+        root(1, every_tile)
+        transpose_scale(0, 1)
+        broadcast_bias(0)
+        quantise(0, 0)
+        scale_and_shift(1, every_tile)
+        quantise(0, 1)
+
+        standardise(1, 0)
+        standardise(1, 1)
+        project(0, 0, 0)
+        standardise(1, 2)
+        standardise(1, 3)
+        project(0, 0, 1)
+        broadcast_bias(1)
+        transpose_scale(1, 0)
+        project(0, 1, 0)
+        transpose_scale(1, 1)
+        quantise(1, 0)
+        project(0, 1, 1)
+        broadcast_bias(2)
+        quantise(1, 1)
+        project(0, 2, 0)
+        project(0, 2, 1)
+
+        for w in range(n_weights):
+            for group in range(GROUPS):
+                project(1, w, group)

@@ -179,7 +179,7 @@ def tile_vit_transformerblock_pa_kernel(
                         stop=(g == PASSES - 1),
                     )
                 sums = bank[:].rearrange("p (a d) -> p a d", d=HEAD)
-                if j == 0:
+                if j % 2 == 0:
                     nc.scalar.copy(out=result[:, :, j, :], in_=sums)
                     nc.gpsimd.tensor_tensor(out=result[:, :, j, :], in0=result[:, :, j, :], in1=bias, op=ALU.add)
                 else:

@@ -22,7 +22,9 @@ EPS = 1e-5
 PACK = 4
 K_PASS = P * PACK
 PASSES = FEATURES // K_PASS
-TILES = TOKENS // P
+TILES = 2
+CHUNK = TILES * P
+CHUNKS = BATCHES * TOKENS // CHUNK
 BANK = 512
 BANK_HEADS = BANK // HEAD
 GROUPS = COLUMNS // BANK
@@ -42,10 +44,9 @@ def tile_vit_transformerblock_pa_kernel(
 
     with ExitStack() as ctx:
         keep = ctx.enter_context(tc.tile_pool(name="keep", bufs=1))
-        norm = ctx.enter_context(tc.tile_pool(name="norm", bufs=BATCHES))
-        results = ctx.enter_context(tc.tile_pool(name="results", bufs=4))
+        norm = ctx.enter_context(tc.tile_pool(name="norm", bufs=3))
+        results = ctx.enter_context(tc.tile_pool(name="results", bufs=8))
         banks = ctx.enter_context(tc.psum_pool(name="banks", bufs=8))
-        ctx.enter_context(tc.manual_schedule())
 
         eps = keep.tile([P, 1], F32)
         nc.vector.memset(eps[:], EPS)
@@ -58,23 +59,14 @@ def tile_vit_transformerblock_pa_kernel(
         identity = keep.tile([P, P], F32)
         make_identity(nc, identity[:])
 
-        x_sb = keep.tile([P, BATCHES, TILES, FEATURES], BF16)
-        for b in range(BATCHES):
-            x_tiles = x[b].rearrange("(p j) f -> j p f", j=TILES)
-            for j in range(TILES):
-                nc.sync.dma_start(out=x_sb[:, b, j, :], in_=x_tiles[j])
-
-        gamma_bf = keep.tile([P, PASSES, PACK], BF16)
-        beta_bf = keep.tile([P, PASSES, PACK], BF16)
-        nc.scalar.dma_start(out=gamma_bf[:], in_=gamma.rearrange("(g p t) -> p g t", g=PASSES, t=PACK))
-        nc.scalar.dma_start(out=beta_bf[:], in_=beta.rearrange("(g p t) -> p g t", g=PASSES, t=PACK))
-        table_warm = keep.tile([P, 1], F32)
-        nc.scalar.activation(out=table_warm[:], in_=eps[:], func=ACT.Sqrt)
-        for w in range(n_weights):
-            nc.scalar.dma_start(out=bias_rows[0:1, w, :], in_=weights[w][2].rearrange("(o n) -> o n", o=1))
-
+        x_sb = keep.tile([P, CHUNKS, TILES, FEATURES], BF16)
+        x_chunks = x.rearrange("b (h p j) f -> (b h) p (j f)", p=P, j=TILES)
         w_words = keep.tile([P, n_weights, PASSES, COLUMNS], U32, align_bytes=64)
-        for w in range(n_weights):
+
+        def load_x(c):
+            nc.sync.dma_start(out=x_sb[:, c, :, :].rearrange("p j f -> p (j f)"), in_=x_chunks[c])
+
+        def load_weight(w):
             for quadrant in range(4):
                 rows = slice(4 * quadrant, 4 * quadrant + 4)
                 nc.sync.dma_start(
@@ -86,72 +78,95 @@ def tile_vit_transformerblock_pa_kernel(
                 in_=weights[w][0].rearrange("g p n t -> p g (n t)").bitcast(I32),
             )
 
+        load_x(0)
+        load_x(1)
+        load_weight(0)
+        load_weight(1)
+        load_x(2)
+        load_weight(2)
+        load_x(3)
+
+        gamma_bf = keep.tile([P, PASSES, PACK], BF16)
+        beta_bf = keep.tile([P, PASSES, PACK], BF16)
+        nc.scalar.dma_start(out=gamma_bf[:], in_=gamma.rearrange("(g p t) -> p g t", g=PASSES, t=PACK))
+        nc.scalar.dma_start(out=beta_bf[:], in_=beta.rearrange("(g p t) -> p g t", g=PASSES, t=PACK))
+        table_warm = keep.tile([P, 1], F32)
+        nc.scalar.activation(out=table_warm[:], in_=eps[:], func=ACT.Sqrt)
+        for w in range(n_weights):
+            nc.scalar.dma_start(out=bias_rows[0:1, w, :], in_=weights[w][2].rearrange("(o n) -> o n", o=1))
+
         gamma_f = keep.tile([P, PASSES, PACK], F32)
         beta_f = keep.tile([P, PASSES, PACK], F32)
         bias_all = keep.tile([P, n_weights, COLUMNS], F32)
-        h_words = keep.tile([P, BATCHES, PASSES, TOKENS], U32, align_bytes=64)
-        h_scales = keep.tile([P, BATCHES, PASSES, TOKENS], U8, align_bytes=64)
+        h_words = keep.tile([P, CHUNKS, PASSES, CHUNK], U32, align_bytes=64)
+        h_scales = keep.tile([P, CHUNKS, PASSES, CHUNK], U8, align_bytes=64)
+        of_chunk = {}
 
-        def batch_tiles():
+        def moments(c):
             stats = norm.tile([P, TILES, FEATURES // STATS_MAX, STATS_DIM], F32)
             mean_var = norm.tile([P, TILES, 2], F32)
+            of_chunk[c] = dict(mean_var=mean_var)
+            for j in range(TILES):
+                for s in range(FEATURES // STATS_MAX):
+                    nc.vector.bn_stats(out=stats[:, j, s, :], in_=x_sb[:, c, j, s * STATS_MAX : (s + 1) * STATS_MAX])
+                nc.vector.bn_aggr(out=mean_var[:, j, :], in_=stats[:, j, :, :].rearrange("p s v -> p (s v)"))
+
+        def standardise(c):
+            mean_var = of_chunk[c]["mean_var"]
             std = norm.tile([P, TILES], F32)
             rstd = norm.tile([P, TILES], F32)
             shift = norm.tile([P, TILES], F32)
             z = norm.tile([P, TILES, PACK, FEATURES // PACK], F32)
-            planes = norm.tile([P, PASSES, PACK, TOKENS], BF16)
-            grouped = norm.tile([P, PASSES, TOKENS, PACK], BF16, align_bytes=64)
-            return dict(stats=stats, mean_var=mean_var, std=std, rstd=rstd, shift=shift, z=z, planes=planes, grouped=grouped)
-
-        of_batch = [batch_tiles() for b in range(BATCHES)]
-        every_tile = slice(0, TILES)
-
-        def moments(b, j):
-            t = of_batch[b]
-            for s in range(FEATURES // STATS_MAX):
-                nc.vector.bn_stats(out=t["stats"][:, j, s, :], in_=x_sb[:, b, j, s * STATS_MAX : (s + 1) * STATS_MAX])
-            nc.vector.bn_aggr(out=t["mean_var"][:, j, :], in_=t["stats"][:, j, :, :].rearrange("p s v -> p (s v)"))
-
-        def root(b, tiles):
-            t = of_batch[b]
-            nc.scalar.activation(out=t["std"][:, tiles], in_=t["mean_var"][:, tiles, 1], func=ACT.Sqrt, bias=eps[:], scale=1.0)
-
-        def scale_and_shift(b, tiles):
-            t = of_batch[b]
-            nc.vector.reciprocal(out=t["rstd"][:, tiles], in_=t["std"][:, tiles])
+            of_chunk[c]["z"] = z
+            nc.scalar.activation(out=std[:], in_=mean_var[:, :, 1], func=ACT.Sqrt, bias=eps[:], scale=1.0)
+            nc.vector.reciprocal(out=rstd[:], in_=std[:])
             nc.vector.scalar_tensor_tensor(
-                out=t["shift"][:, tiles], in0=t["mean_var"][:, tiles, 0], scalar=-1.0, in1=t["rstd"][:, tiles],
-                op0=ALU.mult, op1=ALU.mult,
+                out=shift[:], in0=mean_var[:, :, 0], scalar=-1.0, in1=rstd[:], op0=ALU.mult, op1=ALU.mult
             )
-
-        def standardise(b, j):
-            t = of_batch[b]
             nc.scalar.activation(
-                out=t["z"][:, j, :, :], in_=x_sb[:, b, j, :].rearrange("p (c t) -> p t c", t=PACK),
-                func=ACT.Identity, scale=t["rstd"][:, j : j + 1], bias=t["shift"][:, j : j + 1],
+                out=z[:, 0, :, :], in_=x_sb[:, c, 0, :].rearrange("p (i t) -> p t i", t=PACK),
+                func=ACT.Identity, scale=rstd[:, 0:1], bias=shift[:, 0:1],
+            )
+            nc.vector.tensor_scalar(
+                out=z[:, 1, :, :], in0=x_sb[:, c, 1, :].rearrange("p (i t) -> p t i", t=PACK),
+                scalar1=rstd[:, 1:2], scalar2=shift[:, 1:2], op0=ALU.mult, op1=ALU.add,
             )
 
-        def transpose_scale(b, g):
-            tiles = of_batch[b]
-            for t in range(PACK):
-                bank = banks.tile([P, TILES, P], F32, tag="bank")
-                for j in range(TILES):
-                    nc.tensor.transpose(bank[:, j, :], tiles["z"][:, j, t, g * P : (g + 1) * P], identity[:])
+        def transposes(c):
+            z = of_chunk[c]["z"]
+            planes = norm.tile([P, PASSES, PACK, CHUNK], BF16)
+            of_chunk[c]["planes"] = planes
+            of_chunk[c]["banks"] = []
+            for g in range(PASSES):
+                for pair in range(PACK // 2):
+                    bank = banks.tile([P, 2, TILES, P], F32, tag="bank")
+                    of_chunk[c]["banks"].append(bank)
+                    for e in range(2):
+                        for j in range(TILES):
+                            nc.tensor.transpose(bank[:, e, j, :], z[:, j, 2 * pair + e, g * P : (g + 1) * P], identity[:])
+
+        def scale_out(c, n):
+            g, pair = divmod(n, PACK // 2)
+            bank = of_chunk[c]["banks"][n]
+            for e in range(2):
+                t = 2 * pair + e
                 nc.scalar.activation(
-                    out=tiles["planes"][:, g, t, :], in_=bank[:].rearrange("p j m -> p (j m)"), func=ACT.Identity,
-                    scale=gamma_f[:, g, t : t + 1], bias=beta_f[:, g, t : t + 1],
+                    out=of_chunk[c]["planes"][:, g, t, :], in_=bank[:, e, :, :].rearrange("p j m -> p (j m)"),
+                    func=ACT.Identity, scale=gamma_f[:, g, t : t + 1], bias=beta_f[:, g, t : t + 1],
                 )
 
-        def quantise(b, g):
-            tiles = of_batch[b]
-            nc.vector.tensor_copy(
-                out=tiles["grouped"][:, g, :, :].rearrange("p (c i) t -> p c t i", i=4),
-                in_=tiles["planes"][:, g, :, :].rearrange("p t (c i) -> p c t i", i=4),
-            )
+        def quantise(c):
+            planes = of_chunk[c]["planes"]
+            grouped = norm.tile([P, PASSES, CHUNK, PACK], BF16, align_bytes=64)
+            for g in range(PASSES):
+                nc.vector.tensor_copy(
+                    out=grouped[:, g, :, :].rearrange("p (n i) t -> p n t i", i=4),
+                    in_=planes[:, g, :, :].rearrange("p t (n i) -> p n t i", i=4),
+                )
             nc.vector.quantize_mx(
-                out=h_words[:, b, g, :].bitcast(FP8X4),
-                scales=h_scales[:, b, g, :],
-                in_=tiles["grouped"][:, g, :, :].rearrange("p c t -> p (c t)"),
+                out=h_words[:, c, :, :].rearrange("p g m -> p (g m)").bitcast(FP8X4),
+                scales=h_scales[:, c, :, :].rearrange("p g m -> p (g m)"),
+                in_=grouped[:].rearrange("p g m t -> p (g m t)"),
             )
 
         def broadcast_bias(w):
@@ -161,7 +176,7 @@ def tile_vit_transformerblock_pa_kernel(
                 nc.tensor.matmul(out=bank[:], lhsT=ones[:], rhs=bias_rows[:, w, cols], start=True, stop=True)
                 nc.scalar.copy(out=bias_all[:, w, cols], in_=bank[:])
 
-        def project(b, w, group):
+        def project(c, w, group):
             cols = slice(group * BANK, (group + 1) * BANK)
             bias = bias_all[:, w, cols].rearrange("p (a d) -> p a d", d=HEAD)
             result = results.tile([P, BANK_HEADS, TILES, HEAD], F32)
@@ -171,61 +186,53 @@ def tile_vit_transformerblock_pa_kernel(
                 for g in range(PASSES):
                     nc.tensor.matmul_mx(
                         out=bank[:],
-                        lhsT=h_words[:, b, g, tokens].bitcast(FP8X4),
-                        lhsT_scale=h_scales[:, b, g, tokens],
+                        lhsT=h_words[:, c, g, tokens].bitcast(FP8X4),
+                        lhsT_scale=h_scales[:, c, g, tokens],
                         rhs=w_words[:, w, g, cols].bitcast(FP8X4),
                         rhs_scale=w_scales[:, w, g, cols],
                         start=(g == 0),
                         stop=(g == PASSES - 1),
                     )
                 sums = bank[:].rearrange("p (a d) -> p a d", d=HEAD)
-                if j % 2 == 0:
+                if j == 0:
                     nc.scalar.copy(out=result[:, :, j, :], in_=sums)
                     nc.gpsimd.tensor_tensor(out=result[:, :, j, :], in0=result[:, :, j, :], in1=bias, op=ALU.add)
                 else:
                     nc.vector.tensor_tensor(out=result[:, :, j, :], in0=sums, in1=bias, op=ALU.add)
+            b, half = divmod(c, TOKENS // CHUNK)
             heads = slice(group * BANK_HEADS, (group + 1) * BANK_HEADS)
             nc.sync.dma_start(
-                out=weights[w][3][b, heads].rearrange("a (p j) d -> p a (j d)", j=TILES),
+                out=weights[w][3][b, heads, half * CHUNK : (half + 1) * CHUNK, :].rearrange("a (p j) d -> p a (j d)", j=TILES),
                 in_=result[:].rearrange("p a j d -> p a (j d)"),
             )
 
-        for j in range(TILES + 1):
-            if j < TILES:
-                moments(0, j)
-                root(0, slice(j, j + 1))
-            if j > 0:
-                scale_and_shift(0, slice(j - 1, j))
-                standardise(0, j - 1)
+        units = [(w, group) for w in range(n_weights) for group in range(GROUPS)]
+        n_banks = PASSES * PACK // 2
+
+        broadcast_bias(0)
+        moments(0)
+        standardise(0)
         nc.vector.tensor_copy(out=gamma_f[:], in_=gamma_bf[:])
         nc.vector.tensor_copy(out=beta_f[:], in_=beta_bf[:])
-        for j in range(TILES):
-            moments(1, j)
-        transpose_scale(0, 0)
-        root(1, every_tile)
-        transpose_scale(0, 1)
-        broadcast_bias(0)
-        quantise(0, 0)
-        scale_and_shift(1, every_tile)
-        quantise(0, 1)
+        moments(1)
+        transposes(0)
+        for n in range(n_banks):
+            scale_out(0, n)
+        quantise(0)
+        standardise(1)
 
-        standardise(1, 0)
-        standardise(1, 1)
-        project(0, 0, 0)
-        standardise(1, 2)
-        standardise(1, 3)
-        project(0, 0, 1)
-        broadcast_bias(1)
-        transpose_scale(1, 0)
-        project(0, 1, 0)
-        transpose_scale(1, 1)
-        quantise(1, 0)
-        project(0, 1, 1)
-        broadcast_bias(2)
-        quantise(1, 1)
-        project(0, 2, 0)
-        project(0, 2, 1)
-
-        for w in range(n_weights):
-            for group in range(GROUPS):
-                project(1, w, group)
+        for c in range(CHUNKS):
+            if c + 1 < CHUNKS:
+                transposes(c + 1)
+            for u, (w, group) in enumerate(units):
+                if c == 0 and group == 0 and w > 0:
+                    broadcast_bias(w)
+                if c + 1 < CHUNKS and u < n_banks:
+                    scale_out(c + 1, u)
+                project(c, w, group)
+                if c + 2 < CHUNKS and u == 0:
+                    moments(c + 2)
+                if c + 2 < CHUNKS and u == 2:
+                    standardise(c + 2)
+                if c + 1 < CHUNKS and u == n_banks:
+                    quantise(c + 1)

@@ -31,6 +31,8 @@ GROUPS = COLUMNS // BANK
 STATS_MAX = 512
 STATS_DIM = 6
 
+BY_SCALAR = (6, 6, 2, 2)
+
 FLOPS = 2 * BATCHES * TOKENS * FEATURES * 3 * COLUMNS
 
 
@@ -50,10 +52,10 @@ def tile_vit_transformerblock_pa_kernel(
 
         eps = keep.tile([P, 1], F32)
         nc.vector.memset(eps[:], EPS)
-        bias_rows = keep.tile([P, n_weights, COLUMNS], BF16)
-        nc.vector.memset(bias_rows[:].bitcast(I32), 0)
         w_scales = keep.tile([P, n_weights, PASSES, COLUMNS], U8, align_bytes=64)
-        nc.vector.memset(w_scales[:].bitcast(I32), 0)
+        nc.gpsimd.memset(w_scales[:].bitcast(F32), 0.0)
+        bias_rows = keep.tile([P, n_weights, COLUMNS], BF16)
+        nc.gpsimd.memset(bias_rows[:].bitcast(F32), 0.0)
         ones = keep.tile([P, P], BF16)
         nc.vector.memset(ones[:], 1.0)
         identity = keep.tile([P, P], F32)
@@ -63,8 +65,11 @@ def tile_vit_transformerblock_pa_kernel(
         x_chunks = x.rearrange("b (h p j) f -> (b h) p (j f)", p=P, j=TILES)
         w_words = keep.tile([P, n_weights, PASSES, COLUMNS], U32, align_bytes=64)
 
-        def load_x(c):
-            nc.sync.dma_start(out=x_sb[:, c, :, :].rearrange("p j f -> p (j f)"), in_=x_chunks[c])
+        def load_x(c, pieces=1):
+            width = TILES * FEATURES // pieces
+            for i in range(pieces):
+                part = slice(i * width, (i + 1) * width)
+                nc.sync.dma_start(out=x_sb[:, c, :, :].rearrange("p j f -> p (j f)")[:, part], in_=x_chunks[c][:, part])
 
         def load_weight(w):
             for quadrant in range(4):
@@ -78,7 +83,7 @@ def tile_vit_transformerblock_pa_kernel(
                 in_=weights[w][0].rearrange("g p n t -> p g (n t)").bitcast(I32),
             )
 
-        load_x(0)
+        load_x(0, pieces=TILES * FEATURES // STATS_MAX)
         load_x(1)
         load_weight(0)
         load_weight(1)
@@ -150,23 +155,41 @@ def tile_vit_transformerblock_pa_kernel(
             bank = of_chunk[c]["banks"][n]
             for e in range(2):
                 t = 2 * pair + e
-                nc.scalar.activation(
-                    out=of_chunk[c]["planes"][:, g, t, :], in_=bank[:, e, :, :].rearrange("p j m -> p (j m)"),
-                    func=ACT.Identity, scale=gamma_f[:, g, t : t + 1], bias=beta_f[:, g, t : t + 1],
-                )
+                if c == 0 and pair == 1:
+                    nc.vector.tensor_scalar(
+                        out=of_chunk[c]["planes"][:, g, t, :], in0=bank[:, e, :, :].rearrange("p j m -> p (j m)"),
+                        scalar1=gamma_f[:, g, t : t + 1], scalar2=beta_f[:, g, t : t + 1], op0=ALU.mult, op1=ALU.add,
+                    )
+                else:
+                    nc.scalar.activation(
+                        out=of_chunk[c]["planes"][:, g, t, :], in_=bank[:, e, :, :].rearrange("p j m -> p (j m)"),
+                        func=ACT.Identity, scale=gamma_f[:, g, t : t + 1], bias=beta_f[:, g, t : t + 1],
+                    )
+
+        def interleave(c, g):
+            planes = of_chunk[c]["planes"]
+            if g == 0:
+                grouped = norm.tile([P, PASSES, CHUNK, PACK], BF16, align_bytes=64)
+                of_chunk[c]["grouped"] = grouped
+            nc.vector.tensor_copy(
+                out=of_chunk[c]["grouped"][:, g, :, :].rearrange("p (n i) t -> p n t i", i=4),
+                in_=planes[:, g, :, :].rearrange("p t (n i) -> p n t i", i=4),
+            )
+
+        def quantise_pass(c, g):
+            nc.vector.quantize_mx(
+                out=h_words[:, c, g, :].bitcast(FP8X4),
+                scales=h_scales[:, c, g, :],
+                in_=of_chunk[c]["grouped"][:, g, :, :].rearrange("p m t -> p (m t)"),
+            )
 
         def quantise(c):
-            planes = of_chunk[c]["planes"]
-            grouped = norm.tile([P, PASSES, CHUNK, PACK], BF16, align_bytes=64)
             for g in range(PASSES):
-                nc.vector.tensor_copy(
-                    out=grouped[:, g, :, :].rearrange("p (n i) t -> p n t i", i=4),
-                    in_=planes[:, g, :, :].rearrange("p t (n i) -> p n t i", i=4),
-                )
+                interleave(c, g)
             nc.vector.quantize_mx(
                 out=h_words[:, c, :, :].rearrange("p g m -> p (g m)").bitcast(FP8X4),
                 scales=h_scales[:, c, :, :].rearrange("p g m -> p (g m)"),
-                in_=grouped[:].rearrange("p g m t -> p (g m t)"),
+                in_=of_chunk[c]["grouped"][:].rearrange("p g m t -> p (g m t)"),
             )
 
         def broadcast_bias(w):
@@ -180,21 +203,28 @@ def tile_vit_transformerblock_pa_kernel(
             cols = slice(group * BANK, (group + 1) * BANK)
             bias = bias_all[:, w, cols].rearrange("p (a d) -> p a d", d=HEAD)
             result = results.tile([P, BANK_HEADS, TILES, HEAD], F32)
+            unit_banks = []
             for j in range(TILES):
-                tokens = slice(j * P, (j + 1) * P)
                 bank = banks.tile([P, BANK], F32, tag="bank")
-                for g in range(PASSES):
-                    nc.tensor.matmul_mx(
-                        out=bank[:],
-                        lhsT=h_words[:, c, g, tokens].bitcast(FP8X4),
-                        lhsT_scale=h_scales[:, c, g, tokens],
-                        rhs=w_words[:, w, g, cols].bitcast(FP8X4),
-                        rhs_scale=w_scales[:, w, g, cols],
-                        start=(g == 0),
-                        stop=(g == PASSES - 1),
-                    )
-                sums = bank[:].rearrange("p (a d) -> p a d", d=HEAD)
-                if j == 0:
+                unit_banks.append(bank)
+            if c == 0:
+                passes = [(j, g) for g in range(PASSES) for j in range(TILES)]
+            else:
+                passes = [(j, g) for j in range(TILES) for g in range(PASSES)]
+            for j, g in passes:
+                tokens = slice(j * P, (j + 1) * P)
+                nc.tensor.matmul_mx(
+                    out=unit_banks[j][:],
+                    lhsT=h_words[:, c, g, tokens].bitcast(FP8X4),
+                    lhsT_scale=h_scales[:, c, g, tokens],
+                    rhs=w_words[:, w, g, cols].bitcast(FP8X4),
+                    rhs_scale=w_scales[:, w, g, cols],
+                    start=(g == 0),
+                    stop=(g == PASSES - 1),
+                )
+            for j in range(TILES):
+                sums = unit_banks[j][:].rearrange("p (a d) -> p a d", d=HEAD)
+                if j == 0 and GROUPS * w + group < BY_SCALAR[c]:
                     nc.scalar.copy(out=result[:, :, j, :], in_=sums)
                     nc.gpsimd.tensor_tensor(out=result[:, :, j, :], in0=result[:, :, j, :], in1=bias, op=ALU.add)
                 else:
@@ -214,19 +244,21 @@ def tile_vit_transformerblock_pa_kernel(
         standardise(0)
         nc.vector.tensor_copy(out=gamma_f[:], in_=gamma_bf[:])
         nc.vector.tensor_copy(out=beta_f[:], in_=beta_bf[:])
-        moments(1)
         transposes(0)
-        for n in range(n_banks):
-            scale_out(0, n)
-        quantise(0)
+        for g in range(PASSES):
+            for pair in range(PACK // 2):
+                scale_out(0, g * (PACK // 2) + pair)
+            interleave(0, g)
+            quantise_pass(0, g)
+        for w in range(1, n_weights):
+            broadcast_bias(w)
+        moments(1)
         standardise(1)
 
         for c in range(CHUNKS):
             if c + 1 < CHUNKS:
                 transposes(c + 1)
             for u, (w, group) in enumerate(units):
-                if c == 0 and group == 0 and w > 0:
-                    broadcast_bias(w)
                 if c + 1 < CHUNKS and u < n_banks:
                     scale_out(c + 1, u)
                 project(c, w, group)

@@ -31,7 +31,9 @@ GROUPS = COLUMNS // BANK
 STATS_MAX = 512
 STATS_DIM = 6
 
-BY_SCALAR = (6, 6, 2, 2)
+BY_SCALAR = ((2, 6), (0, 6), (0, 2), (0, 2))
+
+WARM_UP = 12
 
 FLOPS = 2 * BATCHES * TOKENS * FEATURES * 3 * COLUMNS
 
@@ -128,10 +130,17 @@ def tile_vit_transformerblock_pa_kernel(
             nc.vector.scalar_tensor_tensor(
                 out=shift[:], in0=mean_var[:, :, 0], scalar=-1.0, in1=rstd[:], op0=ALU.mult, op1=ALU.mult
             )
+            sorted_x = x_sb[:, c, 0, :].rearrange("p (i t) -> p t i", t=PACK)
+            scalar_share = PACK // 2 if c == 0 else PACK
             nc.scalar.activation(
-                out=z[:, 0, :, :], in_=x_sb[:, c, 0, :].rearrange("p (i t) -> p t i", t=PACK),
+                out=z[:, 0, :scalar_share, :], in_=sorted_x[:, :scalar_share, :],
                 func=ACT.Identity, scale=rstd[:, 0:1], bias=shift[:, 0:1],
             )
+            if scalar_share < PACK:
+                nc.gpsimd.tensor_scalar(
+                    out=z[:, 0, scalar_share:, :], in0=sorted_x[:, scalar_share:, :],
+                    scalar1=rstd[:, 0:1], scalar2=shift[:, 0:1], op0=ALU.mult, op1=ALU.add,
+                )
             nc.vector.tensor_scalar(
                 out=z[:, 1, :, :], in0=x_sb[:, c, 1, :].rearrange("p (i t) -> p t i", t=PACK),
                 scalar1=rstd[:, 1:2], scalar2=shift[:, 1:2], op0=ALU.mult, op1=ALU.add,
@@ -146,9 +155,13 @@ def tile_vit_transformerblock_pa_kernel(
                 for pair in range(PACK // 2):
                     bank = banks.tile([P, 2, TILES, P], F32, tag="bank")
                     of_chunk[c]["banks"].append(bank)
-                    for e in range(2):
-                        for j in range(TILES):
-                            nc.tensor.transpose(bank[:, e, j, :], z[:, j, 2 * pair + e, g * P : (g + 1) * P], identity[:])
+            if c == 0:
+                order = [(n, e, j) for j in reversed(range(TILES)) for n in range(PASSES * PACK // 2) for e in range(2)]
+            else:
+                order = [(n, e, j) for n in range(PASSES * PACK // 2) for e in range(2) for j in range(TILES)]
+            for n, e, j in order:
+                g, pair = divmod(n, PACK // 2)
+                nc.tensor.transpose(of_chunk[c]["banks"][n][:, e, j, :], z[:, j, 2 * pair + e, g * P : (g + 1) * P], identity[:])
 
         def scale_out(c, n):
             g, pair = divmod(n, PACK // 2)
@@ -224,7 +237,7 @@ def tile_vit_transformerblock_pa_kernel(
                 )
             for j in range(TILES):
                 sums = unit_banks[j][:].rearrange("p (a d) -> p a d", d=HEAD)
-                if j == 0 and GROUPS * w + group < BY_SCALAR[c]:
+                if j == 0 and BY_SCALAR[c][0] <= GROUPS * w + group < BY_SCALAR[c][1]:
                     nc.scalar.copy(out=result[:, :, j, :], in_=sums)
                     nc.gpsimd.tensor_tensor(out=result[:, :, j, :], in0=result[:, :, j, :], in1=bias, op=ALU.add)
                 else:
@@ -239,7 +252,12 @@ def tile_vit_transformerblock_pa_kernel(
         units = [(w, group) for w in range(n_weights) for group in range(GROUPS)]
         n_banks = PASSES * PACK // 2
 
-        broadcast_bias(0)
+        warm = banks.tile([P, BANK], F32, tag="bank")
+        for i in range(WARM_UP):
+            j, s = divmod(i % (TILES * FEATURES // STATS_MAX), FEATURES // STATS_MAX)
+            nc.tensor.matmul(
+                out=warm[:], lhsT=ones[:], rhs=x_sb[:, 0, j, s * STATS_MAX : (s + 1) * STATS_MAX], start=True, stop=True
+            )
         moments(0)
         standardise(0)
         nc.vector.tensor_copy(out=gamma_f[:], in_=gamma_bf[:])
@@ -250,7 +268,7 @@ def tile_vit_transformerblock_pa_kernel(
                 scale_out(0, g * (PACK // 2) + pair)
             interleave(0, g)
             quantise_pass(0, g)
-        for w in range(1, n_weights):
+        for w in range(n_weights):
             broadcast_bias(w)
         moments(1)
         standardise(1)

@@ -244,7 +244,8 @@ def tile_vit_transformerblock_pa_kernel(
                     nc.vector.tensor_tensor(out=result[:, :, j, :], in0=sums, in1=bias, op=ALU.add)
             b, half = divmod(c, TOKENS // CHUNK)
             heads = slice(group * BANK_HEADS, (group + 1) * BANK_HEADS)
-            nc.sync.dma_start(
+            queue = nc.scalar if c >= CHUNKS - 2 and group == 1 else nc.sync
+            queue.dma_start(
                 out=weights[w][3][b, heads, half * CHUNK : (half + 1) * CHUNK, :].rearrange("a (p j) d -> p a (j d)", j=TILES),
                 in_=result[:].rearrange("p a j d -> p a (j d)"),
             )

@@ -25,6 +25,7 @@ PASSES = FEATURES // K_PASS
 TILES = 2
 CHUNK = TILES * P
 CHUNKS = BATCHES * TOKENS // CHUNK
+HALVES = TOKENS // CHUNK
 BANK = 512
 BANK_HEADS = BANK // HEAD
 GROUPS = COLUMNS // BANK
@@ -32,6 +33,8 @@ STATS_MAX = 512
 STATS_DIM = 6
 
 BY_SCALAR = ((2, 6), (0, 6), (0, 2), (0, 2))
+
+FIRST_WHOLE = (5, 4)
 
 WARM_UP = 12
 
@@ -64,7 +67,8 @@ def tile_vit_transformerblock_pa_kernel(
         make_identity(nc, identity[:])
 
         x_sb = keep.tile([P, CHUNKS, TILES, FEATURES], BF16)
-        x_chunks = x.rearrange("b (h p j) f -> (b h) p (j f)", p=P, j=TILES)
+        x_halves = x.rearrange("b (p h j) f -> b h p (j f)", h=HALVES, j=TILES)
+        x_chunks = [x_halves[c // HALVES, c % HALVES] for c in range(CHUNKS)]
         w_words = keep.tile([P, n_weights, PASSES, COLUMNS], U32, align_bytes=64)
 
         def load_x(c, pieces=1):
@@ -212,10 +216,20 @@ def tile_vit_transformerblock_pa_kernel(
                 nc.tensor.matmul(out=bank[:], lhsT=ones[:], rhs=bias_rows[:, w, cols], start=True, stop=True)
                 nc.scalar.copy(out=bias_all[:, w, cols], in_=bank[:])
 
-        def project(c, w, group):
+        def project(c, place, u):
+            w, group = units[u]
             cols = slice(group * BANK, (group + 1) * BANK)
             bias = bias_all[:, w, cols].rearrange("p (a d) -> p a d", d=HEAD)
-            result = results.tile([P, BANK_HEADS, TILES, HEAD], F32)
+            b, half = divmod(c, HALVES)
+            whole = u >= FIRST_WHOLE[b]
+            if not whole:
+                held = results.tile([P, BANK_HEADS, 1, TILES, HEAD], F32, tag="one")
+            elif half == 0:
+                held = results.tile([P, BANK_HEADS, HALVES, TILES, HEAD], F32, bufs=4)
+                of_unit[b, u] = held
+            else:
+                held = of_unit[b, u]
+            result = held[:, :, half if whole else 0, :, :]
             unit_banks = []
             for j in range(TILES):
                 bank = banks.tile([P, BANK], F32, tag="bank")
@@ -237,20 +251,23 @@ def tile_vit_transformerblock_pa_kernel(
                 )
             for j in range(TILES):
                 sums = unit_banks[j][:].rearrange("p (a d) -> p a d", d=HEAD)
-                if j == 0 and BY_SCALAR[c][0] <= GROUPS * w + group < BY_SCALAR[c][1]:
+                if j == 0 and BY_SCALAR[c][0] <= place < BY_SCALAR[c][1]:
                     nc.scalar.copy(out=result[:, :, j, :], in_=sums)
                     nc.gpsimd.tensor_tensor(out=result[:, :, j, :], in0=result[:, :, j, :], in1=bias, op=ALU.add)
                 else:
                     nc.vector.tensor_tensor(out=result[:, :, j, :], in0=sums, in1=bias, op=ALU.add)
-            b, half = divmod(c, TOKENS // CHUNK)
+            if whole and half < HALVES - 1:
+                return
             heads = slice(group * BANK_HEADS, (group + 1) * BANK_HEADS)
             queue = nc.scalar if c >= CHUNKS - 2 and group == 1 else nc.sync
+            tokens_of = weights[w][3][b, heads, :, :].rearrange("a (p h j) d -> p a h (j d)", h=HALVES, j=TILES)
             queue.dma_start(
-                out=weights[w][3][b, heads, half * CHUNK : (half + 1) * CHUNK, :].rearrange("a (p j) d -> p a (j d)", j=TILES),
-                in_=result[:].rearrange("p a j d -> p a (j d)"),
+                out=tokens_of.rearrange("p a h e -> p a (h e)") if whole else tokens_of[:, :, half, :],
+                in_=held[:].rearrange("p a h j d -> p a (h j d)"),
             )
 
         units = [(w, group) for w in range(n_weights) for group in range(GROUPS)]
+        of_unit = {}
         n_banks = PASSES * PACK // 2
 
         warm = banks.tile([P, BANK], F32, tag="bank")
@@ -274,16 +291,22 @@ def tile_vit_transformerblock_pa_kernel(
         moments(1)
         standardise(1)
 
-        for c in range(CHUNKS):
-            if c + 1 < CHUNKS:
-                transposes(c + 1)
-            for u, (w, group) in enumerate(units):
-                if c + 1 < CHUNKS and u < n_banks:
-                    scale_out(c + 1, u)
-                project(c, w, group)
-                if c + 2 < CHUNKS and u == 0:
+        for b in range(BATCHES):
+            first, second = HALVES * b, HALVES * b + 1
+            k = FIRST_WHOLE[b]
+            turns = [(first, u, u) for u in range(k)]
+            for u in range(k, len(units)):
+                turns += [(first, u, u), (second, u - k, u)]
+            turns += [(second, len(units) - k + u, u) for u in range(k)]
+            for c, place, u in turns:
+                if c + 1 < CHUNKS and place == 0:
+                    transposes(c + 1)
+                if c + 1 < CHUNKS and place < n_banks:
+                    scale_out(c + 1, place)
+                project(c, place, u)
+                if c + 2 < CHUNKS and place == 0:
                     moments(c + 2)
-                if c + 2 < CHUNKS and u == 2:
+                if c + 2 < CHUNKS and place == 2:
                     standardise(c + 2)
-                if c + 1 < CHUNKS and u == n_banks:
+                if c + 1 < CHUNKS and place == min(n_banks, FIRST_WHOLE[b]):
                     quantise(c + 1)

@@ -55,6 +55,8 @@ def tile_vit_transformerblock_pa_kernel(
         results = ctx.enter_context(tc.tile_pool(name="results", bufs=8))
         banks = ctx.enter_context(tc.psum_pool(name="banks", bufs=8))
 
+        ctx.enter_context(tc.manual_schedule(engines={mybir.EngineType.SP}))
+
         eps = keep.tile([P, 1], F32)
         nc.vector.memset(eps[:], EPS)
         w_scales = keep.tile([P, n_weights, PASSES, COLUMNS], U8, align_bytes=64)
@@ -95,7 +97,6 @@ def tile_vit_transformerblock_pa_kernel(
         load_weight(1)
         load_x(2)
         load_weight(2)
-        load_x(3)
 
         gamma_bf = keep.tile([P, PASSES, PACK], BF16)
         beta_bf = keep.tile([P, PASSES, PACK], BF16)
@@ -304,6 +305,8 @@ def tile_vit_transformerblock_pa_kernel(
                 if c + 1 < CHUNKS and place < n_banks:
                     scale_out(c + 1, place)
                 project(c, place, u)
+                if (c, place) == (0, 1):
+                    load_x(3)
                 if c + 2 < CHUNKS and place == 0:
                     moments(c + 2)
                 if c + 2 < CHUNKS and place == 2:

from contextlib import ExitStack

import concourse.mybir as mybir
from concourse.masks import make_identity

F32 = mybir.dt.float32
BF16 = mybir.dt.bfloat16
I32 = mybir.dt.int32
U32 = mybir.dt.uint32
U8 = mybir.dt.uint8
FP8X4 = mybir.dt.float8_e4m3fn_x4
ALU = mybir.AluOpType
ACT = mybir.ActivationFunctionType

P = 128
BATCHES = 2
TOKENS = 512
FEATURES = 1024
COLUMNS = 1024
HEAD = 128
EPS = 1e-5
PACK = 4
K_PASS = P * PACK
PASSES = FEATURES // K_PASS
TILES = 2
CHUNK = TILES * P
CHUNKS = BATCHES * TOKENS // CHUNK
HALVES = TOKENS // CHUNK
BANK = 512
BANK_HEADS = BANK // HEAD
GROUPS = COLUMNS // BANK
STATS_MAX = 512
STATS_DIM = 6

BY_SCALAR = ((2, 6), (0, 6), (0, 2), (0, 2))

FIRST_WHOLE = (5, 4)

WARM_UP = 12

FLOPS = 2 * BATCHES * TOKENS * FEATURES * 3 * COLUMNS


def tile_vit_transformerblock_pa_kernel(
    tc, x, gamma, beta, Wq_words, Wq_scales, bq, Wk_words, Wk_scales, bk, Wv_words, Wv_scales, bv,
    out_0, out_1, out_2,
):
    nc = tc.nc
    weights = ((Wq_words, Wq_scales, bq, out_0), (Wk_words, Wk_scales, bk, out_1), (Wv_words, Wv_scales, bv, out_2))
    n_weights = len(weights)

    with ExitStack() as ctx:
        keep = ctx.enter_context(tc.tile_pool(name="keep", bufs=1))
        norm = ctx.enter_context(tc.tile_pool(name="norm", bufs=3))
        results = ctx.enter_context(tc.tile_pool(name="results", bufs=8))
        banks = ctx.enter_context(tc.psum_pool(name="banks", bufs=8))

        ctx.enter_context(tc.manual_schedule(engines={mybir.EngineType.SP}))

        eps = keep.tile([P, 1], F32)
        nc.vector.memset(eps[:], EPS)
        w_scales = keep.tile([P, n_weights, PASSES, COLUMNS], U8, align_bytes=64)
        nc.gpsimd.memset(w_scales[:].bitcast(F32), 0.0)
        bias_rows = keep.tile([P, n_weights, COLUMNS], BF16)
        nc.gpsimd.memset(bias_rows[:].bitcast(F32), 0.0)
        ones = keep.tile([P, P], BF16)
        nc.vector.memset(ones[:], 1.0)
        identity = keep.tile([P, P], F32)
        make_identity(nc, identity[:])

        x_sb = keep.tile([P, CHUNKS, TILES, FEATURES], BF16)
        x_halves = x.rearrange("b (p h j) f -> b h p (j f)", h=HALVES, j=TILES)
        x_chunks = [x_halves[c // HALVES, c % HALVES] for c in range(CHUNKS)]
        w_words = keep.tile([P, n_weights, PASSES, COLUMNS], U32, align_bytes=64)

        def load_x(c, pieces=1):
            width = TILES * FEATURES // pieces
            for i in range(pieces):
                part = slice(i * width, (i + 1) * width)
                nc.sync.dma_start(out=x_sb[:, c, :, :].rearrange("p j f -> p (j f)")[:, part], in_=x_chunks[c][:, part])

        def load_weight(w):
            for quadrant in range(4):
                rows = slice(4 * quadrant, 4 * quadrant + 4)
                nc.sync.dma_start(
                    out=w_scales[32 * quadrant : 32 * quadrant + 4, w, :, :].bitcast(I32),
                    in_=weights[w][1][:, rows, :].rearrange("g r n -> r g n").bitcast(I32),
                )
            nc.sync.dma_start(
                out=w_words[:, w, :, :].bitcast(I32),
                in_=weights[w][0].rearrange("g p n t -> p g (n t)").bitcast(I32),
            )

        load_x(0, pieces=TILES * FEATURES // STATS_MAX)
        load_x(1)
        load_weight(0)
        load_weight(1)
        load_x(2)
        load_weight(2)

        gamma_bf = keep.tile([P, PASSES, PACK], BF16)
        beta_bf = keep.tile([P, PASSES, PACK], BF16)
        nc.scalar.dma_start(out=gamma_bf[:], in_=gamma.rearrange("(g p t) -> p g t", g=PASSES, t=PACK))
        nc.scalar.dma_start(out=beta_bf[:], in_=beta.rearrange("(g p t) -> p g t", g=PASSES, t=PACK))
        table_warm = keep.tile([P, 1], F32)
        nc.scalar.activation(out=table_warm[:], in_=eps[:], func=ACT.Sqrt)
        for w in range(n_weights):
            nc.scalar.dma_start(out=bias_rows[0:1, w, :], in_=weights[w][2].rearrange("(o n) -> o n", o=1))

        gamma_f = keep.tile([P, PASSES, PACK], F32)
        beta_f = keep.tile([P, PASSES, PACK], F32)
        bias_all = keep.tile([P, n_weights, COLUMNS], F32)
        h_words = keep.tile([P, CHUNKS, PASSES, CHUNK], U32, align_bytes=64)
        h_scales = keep.tile([P, CHUNKS, PASSES, CHUNK], U8, align_bytes=64)
        of_chunk = {}

        def moments(c):
            stats = norm.tile([P, TILES, FEATURES // STATS_MAX, STATS_DIM], F32)
            mean_var = norm.tile([P, TILES, 2], F32)
            of_chunk[c] = dict(mean_var=mean_var)
            for j in range(TILES):
                for s in range(FEATURES // STATS_MAX):
                    nc.vector.bn_stats(out=stats[:, j, s, :], in_=x_sb[:, c, j, s * STATS_MAX : (s + 1) * STATS_MAX])
                nc.vector.bn_aggr(out=mean_var[:, j, :], in_=stats[:, j, :, :].rearrange("p s v -> p (s v)"))

        def standardise(c):
            mean_var = of_chunk[c]["mean_var"]
            std = norm.tile([P, TILES], F32)
            rstd = norm.tile([P, TILES], F32)
            shift = norm.tile([P, TILES], F32)
            z = norm.tile([P, TILES, PACK, FEATURES // PACK], F32)
            of_chunk[c]["z"] = z
            nc.scalar.activation(out=std[:], in_=mean_var[:, :, 1], func=ACT.Sqrt, bias=eps[:], scale=1.0)
            nc.vector.reciprocal(out=rstd[:], in_=std[:])
            nc.vector.scalar_tensor_tensor(
                out=shift[:], in0=mean_var[:, :, 0], scalar=-1.0, in1=rstd[:], op0=ALU.mult, op1=ALU.mult
            )
            sorted_x = x_sb[:, c, 0, :].rearrange("p (i t) -> p t i", t=PACK)
            scalar_share = PACK // 2 if c == 0 else PACK
            nc.scalar.activation(
                out=z[:, 0, :scalar_share, :], in_=sorted_x[:, :scalar_share, :],
                func=ACT.Identity, scale=rstd[:, 0:1], bias=shift[:, 0:1],
            )
            if scalar_share < PACK:
                nc.gpsimd.tensor_scalar(
                    out=z[:, 0, scalar_share:, :], in0=sorted_x[:, scalar_share:, :],
                    scalar1=rstd[:, 0:1], scalar2=shift[:, 0:1], op0=ALU.mult, op1=ALU.add,
                )
            nc.vector.tensor_scalar(
                out=z[:, 1, :, :], in0=x_sb[:, c, 1, :].rearrange("p (i t) -> p t i", t=PACK),
                scalar1=rstd[:, 1:2], scalar2=shift[:, 1:2], op0=ALU.mult, op1=ALU.add,
            )

        def transposes(c):
            z = of_chunk[c]["z"]
            planes = norm.tile([P, PASSES, PACK, CHUNK], BF16)
            of_chunk[c]["planes"] = planes
            of_chunk[c]["banks"] = []
            for g in range(PASSES):
                for pair in range(PACK // 2):
                    bank = banks.tile([P, 2, TILES, P], F32, tag="bank")
                    of_chunk[c]["banks"].append(bank)
            if c == 0:
                order = [(n, e, j) for j in reversed(range(TILES)) for n in range(PASSES * PACK // 2) for e in range(2)]
            else:
                order = [(n, e, j) for n in range(PASSES * PACK // 2) for e in range(2) for j in range(TILES)]
            for n, e, j in order:
                g, pair = divmod(n, PACK // 2)
                nc.tensor.transpose(of_chunk[c]["banks"][n][:, e, j, :], z[:, j, 2 * pair + e, g * P : (g + 1) * P], identity[:])

        def scale_out(c, n):
            g, pair = divmod(n, PACK // 2)
            bank = of_chunk[c]["banks"][n]
            for e in range(2):
                t = 2 * pair + e
                if c == 0 and pair == 1:
                    nc.vector.tensor_scalar(
                        out=of_chunk[c]["planes"][:, g, t, :], in0=bank[:, e, :, :].rearrange("p j m -> p (j m)"),
                        scalar1=gamma_f[:, g, t : t + 1], scalar2=beta_f[:, g, t : t + 1], op0=ALU.mult, op1=ALU.add,
                    )
                else:
                    nc.scalar.activation(
                        out=of_chunk[c]["planes"][:, g, t, :], in_=bank[:, e, :, :].rearrange("p j m -> p (j m)"),
                        func=ACT.Identity, scale=gamma_f[:, g, t : t + 1], bias=beta_f[:, g, t : t + 1],
                    )

        def interleave(c, g):
            planes = of_chunk[c]["planes"]
            if g == 0:
                grouped = norm.tile([P, PASSES, CHUNK, PACK], BF16, align_bytes=64)
                of_chunk[c]["grouped"] = grouped
            nc.vector.tensor_copy(
                out=of_chunk[c]["grouped"][:, g, :, :].rearrange("p (n i) t -> p n t i", i=4),
                in_=planes[:, g, :, :].rearrange("p t (n i) -> p n t i", i=4),
            )

        def quantise_pass(c, g):
            nc.vector.quantize_mx(
                out=h_words[:, c, g, :].bitcast(FP8X4),
                scales=h_scales[:, c, g, :],
                in_=of_chunk[c]["grouped"][:, g, :, :].rearrange("p m t -> p (m t)"),
            )

        def quantise(c):
            for g in range(PASSES):
                interleave(c, g)
            nc.vector.quantize_mx(
                out=h_words[:, c, :, :].rearrange("p g m -> p (g m)").bitcast(FP8X4),
                scales=h_scales[:, c, :, :].rearrange("p g m -> p (g m)"),
                in_=of_chunk[c]["grouped"][:].rearrange("p g m t -> p (g m t)"),
            )

        def broadcast_bias(w):
            for group in range(GROUPS):
                cols = slice(group * BANK, (group + 1) * BANK)
                bank = banks.tile([P, BANK], F32, tag="bank")
                nc.tensor.matmul(out=bank[:], lhsT=ones[:], rhs=bias_rows[:, w, cols], start=True, stop=True)
                nc.scalar.copy(out=bias_all[:, w, cols], in_=bank[:])

        def project(c, place, u):
            w, group = units[u]
            cols = slice(group * BANK, (group + 1) * BANK)
            bias = bias_all[:, w, cols].rearrange("p (a d) -> p a d", d=HEAD)
            b, half = divmod(c, HALVES)
            whole = u >= FIRST_WHOLE[b]
            if not whole:
                held = results.tile([P, BANK_HEADS, 1, TILES, HEAD], F32, tag="one")
            elif half == 0:
                held = results.tile([P, BANK_HEADS, HALVES, TILES, HEAD], F32, bufs=4)
                of_unit[b, u] = held
            else:
                held = of_unit[b, u]
            result = held[:, :, half if whole else 0, :, :]
            unit_banks = []
            for j in range(TILES):
                bank = banks.tile([P, BANK], F32, tag="bank")
                unit_banks.append(bank)
            if c == 0:
                passes = [(j, g) for g in range(PASSES) for j in range(TILES)]
            else:
                passes = [(j, g) for j in range(TILES) for g in range(PASSES)]
            for j, g in passes:
                tokens = slice(j * P, (j + 1) * P)
                nc.tensor.matmul_mx(
                    out=unit_banks[j][:],
                    lhsT=h_words[:, c, g, tokens].bitcast(FP8X4),
                    lhsT_scale=h_scales[:, c, g, tokens],
                    rhs=w_words[:, w, g, cols].bitcast(FP8X4),
                    rhs_scale=w_scales[:, w, g, cols],
                    start=(g == 0),
                    stop=(g == PASSES - 1),
                )
            for j in range(TILES):
                sums = unit_banks[j][:].rearrange("p (a d) -> p a d", d=HEAD)
                if j == 0 and BY_SCALAR[c][0] <= place < BY_SCALAR[c][1]:
                    nc.scalar.copy(out=result[:, :, j, :], in_=sums)
                    nc.gpsimd.tensor_tensor(out=result[:, :, j, :], in0=result[:, :, j, :], in1=bias, op=ALU.add)
                else:
                    nc.vector.tensor_tensor(out=result[:, :, j, :], in0=sums, in1=bias, op=ALU.add)
            if whole and half < HALVES - 1:
                return
            heads = slice(group * BANK_HEADS, (group + 1) * BANK_HEADS)
            queue = nc.scalar if c >= CHUNKS - 2 and group == 1 else nc.sync
            tokens_of = weights[w][3][b, heads, :, :].rearrange("a (p h j) d -> p a h (j d)", h=HALVES, j=TILES)
            queue.dma_start(
                out=tokens_of.rearrange("p a h e -> p a (h e)") if whole else tokens_of[:, :, half, :],
                in_=held[:].rearrange("p a h j d -> p a (h j d)"),
            )

        units = [(w, group) for w in range(n_weights) for group in range(GROUPS)]
        of_unit = {}
        n_banks = PASSES * PACK // 2

        warm = banks.tile([P, BANK], F32, tag="bank")
        for i in range(WARM_UP):
            j, s = divmod(i % (TILES * FEATURES // STATS_MAX), FEATURES // STATS_MAX)
            nc.tensor.matmul(
                out=warm[:], lhsT=ones[:], rhs=x_sb[:, 0, j, s * STATS_MAX : (s + 1) * STATS_MAX], start=True, stop=True
            )
        moments(0)
        standardise(0)
        nc.vector.tensor_copy(out=gamma_f[:], in_=gamma_bf[:])
        nc.vector.tensor_copy(out=beta_f[:], in_=beta_bf[:])
        transposes(0)
        for g in range(PASSES):
            for pair in range(PACK // 2):
                scale_out(0, g * (PACK // 2) + pair)
            interleave(0, g)
            quantise_pass(0, g)
        for w in range(n_weights):
            broadcast_bias(w)
        moments(1)
        standardise(1)

        for b in range(BATCHES):
            first, second = HALVES * b, HALVES * b + 1
            k = FIRST_WHOLE[b]
            turns = [(first, u, u) for u in range(k)]
            for u in range(k, len(units)):
                turns += [(first, u, u), (second, u - k, u)]
            turns += [(second, len(units) - k + u, u) for u in range(k)]
            for c, place, u in turns:
                if c + 1 < CHUNKS and place == 0:
                    transposes(c + 1)
                if c + 1 < CHUNKS and place < n_banks:
                    scale_out(c + 1, place)
                project(c, place, u)
                if (c, place) == (0, 1):
                    load_x(3)
                if c + 2 < CHUNKS and place == 0:
                    moments(c + 2)
                if c + 2 < CHUNKS and place == 2:
                    standardise(c + 2)
                if c + 1 < CHUNKS and place == min(n_banks, FIRST_WHOLE[b]):
                    quantise(c + 1)
